import numpy as np
import ml_dtypes


def mxq(x, axis, fmt="e4m3"):
    dtype, down = {"e4m3": (ml_dtypes.float8_e4m3fn, 7), "e5m2": (ml_dtypes.float8_e5m2, 14)}[fmt]
    v = np.moveaxis(np.asarray(x, np.float32).astype(ml_dtypes.bfloat16).astype(np.float64), axis, -1)
    blocks = v.reshape(v.shape[:-1] + (-1, 32))
    amax = np.abs(blocks).max(-1, keepdims=True)
    byte = np.maximum(np.where(amax > 0, np.frexp(amax)[1] - 1 + 127, 0) - down, 1)
    scale = np.exp2(byte - 127.0)
    codes = (blocks / scale).astype(np.float32).astype(dtype).astype(np.float64)
    return np.moveaxis((codes * scale).reshape(v.shape), -1, axis)


WIDE = False


def mx_kscale(k):
    if not WIDE:
        return np.ones(k)
    levels = np.array([10, -10, 5, -5, 0])
    a = np.random.permutation(np.resize(levels, k // 512 * 4)).reshape(k // 512, 4)
    idx = np.arange(k)
    return np.exp2(a[idx // 512, idx % 128 // 32])


BF16 = ml_dtypes.bfloat16


def bf(x):
    return np.asarray(x, np.float32).astype(BF16)


def f64(x):
    return np.asarray(x).astype(np.float64)


E2M1 = np.array([0.0, 0.5, 1.0, 1.5, 2.0, 3.0, 4.0, 6.0, -0.0, -0.5, -1.0, -1.5, -2.0, -3.0, -4.0, -6.0])


def pack_weight(w, fmt):
    k, n = w.shape
    w = f64(bf(w)).reshape(k // 32, 32, n)
    amax = np.abs(w).max(1)
    if fmt == "e4m3":
        byte = np.frexp(amax)[1] - 1 + 127 - 7
    else:
        mant, ex = np.frexp(amax / 6.0)
        byte = np.where(mant > 0.5, ex, ex - 1) + 127
    byte = np.clip(np.where(amax > 0, byte, 1), 1, 254)
    scaled = (w * np.exp2(127.0 - byte)[:, None, :]).reshape(k, n).astype(np.float32)
    by_word = np.ascontiguousarray(scaled.reshape(k // 512, 128, 4, n).transpose(0, 1, 3, 2))
    if fmt == "e4m3":
        words = by_word.astype(ml_dtypes.float8_e4m3fn).view(np.uint8)
    else:
        c = by_word.astype(ml_dtypes.float4_e2m1fn).view(np.uint8) & 0xF
        words = c[..., 0::2] | (c[..., 1::2] << 4)
    return np.ascontiguousarray(words), np.ascontiguousarray(byte.astype(np.uint8).reshape(k // 512, 16, n))


def unpack_weight(words, scales, fmt):
    g, p, n, _ = words.shape
    if fmt == "e4m3":
        vals = np.ascontiguousarray(words).view(ml_dtypes.float8_e4m3fn).astype(np.float64)
    else:
        nib = np.empty((g, p, n, 4), np.uint8)
        nib[..., 0::2] = words & 0xF
        nib[..., 1::2] = words >> 4
        vals = E2M1[nib]
    vals = vals * np.repeat(np.exp2(scales.astype(np.float64) - 127.0), 8, axis=1)[..., None]
    return vals.transpose(0, 1, 3, 2).reshape(g * 512, n)


B, S, E, H, DH, ROT, MP = 2, 64, 8192, 8, 128, 32, 4
HD = H * DH
LOC = HD // MP
FMT = "e4m3"


def rope_sincos():
    inv_freq = 1.0 / (10000.0 ** (np.arange(0, ROT, 2) / ROT))
    ang = np.arange(S)[:, None] * inv_freq[None, :]
    return np.sin(ang), np.cos(ang)


def apply_rope(x, sin, cos):
    sin2 = np.repeat(sin, 2, axis=-1)[None, :, None, :]
    cos2 = np.repeat(cos, 2, axis=-1)[None, :, None, :]
    x1 = x[..., ::2]
    x2 = x[..., 1::2]
    rot = np.stack((-x2, x1), axis=-1).reshape(x.shape)
    return x * cos2 + rot * sin2


def setup_inputs():
    s = mx_kscale(E)
    hidden_states = bf(np.random.standard_normal((B, S, E)) * s)
    w = np.random.standard_normal((3 * HD, E)) / np.sqrt(E) / s[None, :]
    words, scales = pack_weight(np.ascontiguousarray(w.T), FMT)
    return {"hidden_states": hidden_states,
            "W_qkv_words": words,
            "W_qkv_scales": scales}


def reference(hidden_states, W_qkv_words, W_qkv_scales):
    qkv = mxq(f64(hidden_states), 2, "e4m3") @ unpack_weight(W_qkv_words, W_qkv_scales, FMT)
    qkv = qkv.reshape(B, S, MP, 3 * LOC)
    q, k, v = np.split(qkv, 3, axis=-1)
    q = q.reshape(B, S, H, DH)
    k = k.reshape(B, S, H, DH)
    v = v.reshape(B, S, H, DH)
    sin, cos = rope_sincos()
    q = np.concatenate([apply_rope(q[..., :ROT], sin, cos), q[..., ROT:]], axis=-1)
    k = np.concatenate([apply_rope(k[..., :ROT], sin, cos), k[..., ROT:]], axis=-1)
    return q, k, v

@@ -1,0 +1,200 @@
+import math
+from contextlib import ExitStack
+
+import concourse.mybir as mybir
+from concourse.masks import make_identity
+
+F32 = mybir.dt.float32
+BF16 = mybir.dt.bfloat16
+I32 = mybir.dt.int32
+U32 = mybir.dt.uint32
+U8 = mybir.dt.uint8
+FP8X4 = mybir.dt.float8_e4m3fn_x4
+ALU = mybir.AluOpType
+ACT = mybir.ActivationFunctionType
+
+P = 128
+POSITIONS = 64
+E = 8192
+K_PASS = 512
+PASSES = E // K_PASS
+HEAD = 128
+ROT = 32
+PAIRS = ROT // 2
+SEGMENT = 256
+KINDS = 3
+V_KIND = 2
+N_ALL = 3072
+BANK = 512
+BANKS = N_ALL // BANK
+PLANES = 4
+QUADRANTS = 4
+ROUND_MAGIC = 1.5 * 2.0**23
+COS = 0
+SIN = 1
+
+FLOPS = 2 * P * E * N_ALL
+
+
+def load_weight_scales(nc, planes, w_scales):
+    nc.vector.memset(planes[:].rearrange("p j n -> p (j n)").bitcast(I32), 0)
+    for j in range(PASSES // PLANES):
+        for quadrant in range(QUADRANTS):
+            first = 32 * quadrant
+            nc.sync.dma_start(
+                out=planes[first : first + 4 * PLANES, j, :].bitcast(I32),
+                in_=w_scales[
+                    PLANES * j : PLANES * (j + 1), 4 * quadrant : 4 * (quadrant + 1), :
+                ].bitcast(I32),
+            )
+
+
+def make_cos_sin(nc, const, cos_sin):
+    token = const.tile([P, 1], I32)
+    nc.gpsimd.iota(token[:], pattern=[[0, 1]], base=0, channel_multiplier=1)
+    position_int = const.tile([P, 1], I32)
+    nc.vector.tensor_single_scalar(
+        out=position_int[:], in_=token[:], scalar=POSITIONS - 1, op=ALU.bitwise_and
+    )
+    position = const.tile([P, 1], F32)
+    nc.vector.tensor_copy(out=position[:], in_=position_int[:])
+
+    turns = const.tile([P, 2, PAIRS], F32)
+    for j in range(PAIRS):
+        turns_per_position = 10000.0 ** (-2.0 * j / ROT) / (2.0 * math.pi)
+        nc.vector.tensor_scalar_mul(
+            out=turns[:, SIN, j : j + 1], in0=position[:], scalar1=turns_per_position
+        )
+    nc.vector.tensor_scalar_add(out=turns[:, COS, :], in0=turns[:, SIN, :], scalar1=0.25)
+    whole_turns = const.tile([P, 2, PAIRS], F32)
+    nc.vector.tensor_scalar(
+        out=whole_turns[:],
+        in0=turns[:],
+        scalar1=ROUND_MAGIC,
+        scalar2=ROUND_MAGIC,
+        op0=ALU.add,
+        op1=ALU.subtract,
+    )
+    part_turn = const.tile([P, 2, PAIRS], F32)
+    nc.vector.tensor_sub(out=part_turn[:], in0=turns[:], in1=whole_turns[:])
+    nc.scalar.activation(out=cos_sin[:], in_=part_turn[:], func=ACT.Sin, scale=2.0 * math.pi)
+
+
+def rotate(nc, work, segment, cos_sin):
+    heads = SEGMENT // HEAD
+    x = segment.rearrange("p (h d) -> p h d", d=HEAD)[:, :, 0:ROT].rearrange(
+        "p h (j e) -> p h j e", e=2
+    )
+    shape = [P, heads, PAIRS, 2]
+    cos = cos_sin[:, COS, :].unsqueeze(1).unsqueeze(3).to_broadcast(shape)
+    sin = cos_sin[:, SIN, :].unsqueeze(1).unsqueeze(3).to_broadcast(shape)
+    x_cos = work.tile(shape, F32)
+    x_sin = work.tile(shape, F32)
+    nc.vector.tensor_mul(out=x_cos[:], in0=x, in1=cos)
+    nc.vector.tensor_mul(out=x_sin[:], in0=x, in1=sin)
+    nc.vector.tensor_sub(out=x[:, :, :, 0], in0=x_cos[:, :, :, 0], in1=x_sin[:, :, :, 1])
+    nc.vector.tensor_add(out=x[:, :, :, 1], in0=x_cos[:, :, :, 1], in1=x_sin[:, :, :, 0])
+
+
+def tile_progenattention_pa_k_kernel(
+    tc, hidden_states, W_qkv_words, W_qkv_scales, out_0, out_1, out_2
+):
+    nc = tc.nc
+    x_dram = hidden_states.flatten_outer_dims()
+    outs = [out.rearrange("b s h d -> (b s) (h d)") for out in (out_0, out_1, out_2)]
+
+    with ExitStack() as pools:
+        const = pools.enter_context(tc.tile_pool(name="const", bufs=1))
+        stage = pools.enter_context(tc.tile_pool(name="stage", bufs=3))
+        w_pool = pools.enter_context(tc.tile_pool(name="w", bufs=8))
+        last_pool = pools.enter_context(tc.tile_pool(name="last", bufs=BANKS))
+        result_pool = pools.enter_context(tc.tile_pool(name="result", bufs=2 * BANKS))
+        work = pools.enter_context(tc.tile_pool(name="work", bufs=4))
+        psum = pools.enter_context(tc.psum_pool(name="psum", bufs=8))
+
+        x_sb = const.tile([P, E], BF16)
+        half = E // 2
+        for i in range(2):
+            columns = slice(half * i, half * (i + 1))
+            nc.sync.dma_start(out=x_sb[:, columns], in_=x_dram[:, columns])
+        planes = const.tile([P, PASSES // PLANES, N_ALL], U8, align_bytes=64)
+        load_weight_scales(nc, planes, W_qkv_scales)
+
+        identity = const.tile([P, P], F32)
+        make_identity(nc, identity[:])
+        cos_sin = const.tile([P, 2, PAIRS], F32)
+        make_cos_sin(nc, const, cos_sin)
+
+        x_words = x_sb[:].bitcast(F32)
+        x_codes = const.tile([P, PASSES * P], U32, align_bytes=64)
+        x_scales = const.tile([P, PASSES * P], U8, align_bytes=64)
+        words_in_pass = K_PASS // 2
+        for i in range(PASSES // 2):
+            transposed = psum.tile([P, 2, 2, P], F32, tag="bank")
+            for g_low in range(2):
+                first_word = words_in_pass * (2 * i + g_low)
+                for u in range(2):
+                    nc.tensor.transpose(
+                        transposed[:, g_low, u, :],
+                        x_words[:, first_word + u : first_word + words_in_pass : 2],
+                        identity[:],
+                    )
+            grouped = stage.tile([P, 2 * K_PASS], BF16, align_bytes=64)
+            nc.scalar.copy(
+                out=grouped[:].bitcast(F32).rearrange("p (g r u) -> p g r u", g=2, u=2),
+                in_=transposed[:].rearrange("p g u r -> p g r u"),
+            )
+            tokens_of_two_passes = slice(2 * P * i, 2 * P * (i + 1))
+            nc.vector.quantize_mx(
+                out=x_codes[:, tokens_of_two_passes].bitcast(FP8X4),
+                scales=x_scales[:, tokens_of_two_passes],
+                in_=grouped[:],
+            )
+
+        banks = []
+        for b in range(BANKS):
+            banks.append(psum.tile([P, BANK], F32, tag="bank", name="qkv_bank%d" % b))
+
+        def mx_pass(g, b, w_codes):
+            j, i = divmod(g, PLANES)
+            tokens = slice(P * g, P * (g + 1))
+            nc.tensor.matmul_mx(
+                out=banks[b][:],
+                lhsT=x_codes[:, tokens].bitcast(FP8X4),
+                lhsT_scale=x_scales[:, tokens],
+                rhs=w_codes.bitcast(FP8X4),
+                rhs_scale=planes[4 * i : P, j, BANK * b : BANK * (b + 1)],
+                start=(g == 0),
+                stop=(g == PASSES - 1),
+            )
+
+        for g in range(PASSES - 1):
+            w_codes = w_pool.tile([P, N_ALL], U32, align_bytes=64)
+            nc.sync.dma_start(
+                out=w_codes[:].bitcast(I32),
+                in_=W_qkv_words[g].rearrange("p n t -> p (n t)").bitcast(I32),
+            )
+            for b in range(BANKS):
+                mx_pass(g, b, w_codes[:, BANK * b : BANK * (b + 1)])
+
+        last_bytes = W_qkv_words[PASSES - 1].rearrange("p n t -> p (n t)")
+        last_codes = []
+        for b in range(BANKS):
+            piece = last_pool.tile([P, BANK], U32, align_bytes=64, name="piece%d" % b, tag="piece")
+            nc.sync.dma_start(
+                out=piece[:].bitcast(I32),
+                in_=last_bytes[:, 4 * BANK * b : 4 * BANK * (b + 1)].bitcast(I32),
+            )
+            last_codes.append(piece)
+
+        for b in range(BANKS):
+            mx_pass(PASSES - 1, b, last_codes[b][:])
+            for s in range(BANK // SEGMENT):
+                group, kind = divmod(b * (BANK // SEGMENT) + s, KINDS)
+                segment = result_pool.tile([P, SEGMENT], F32)
+                nc.scalar.copy(out=segment[:], in_=banks[b][:, SEGMENT * s : SEGMENT * (s + 1)])
+                if kind != V_KIND:
+                    rotate(nc, work, segment[:], cos_sin)
+                nc.sync.dma_start(
+                    out=outs[kind][:, SEGMENT * group : SEGMENT * (group + 1)], in_=segment[:]
+                )

@@ -41,11 +41,11 @@ def load_weight_scales(nc, planes, w_scales):
     for j in range(PASSES // PLANES):
         for quadrant in range(QUADRANTS):
             first = 32 * quadrant
-            nc.sync.dma_start(
-                out=planes[first : first + 4 * PLANES, j, :].bitcast(I32),
+            nc.gpsimd.dma_start(
+                out=planes[first : first + 4 * PLANES, j, :].bitcast(F32),
                 in_=w_scales[
                     PLANES * j : PLANES * (j + 1), 4 * quadrant : 4 * (quadrant + 1), :
-                ].bitcast(I32),
+                ].bitcast(F32),
             )
 
 
@@ -117,11 +117,10 @@ def tile_progenattention_pa_k_kernel(
         for i in range(2):
             columns = slice(half * i, half * (i + 1))
             nc.sync.dma_start(out=x_sb[:, columns], in_=x_dram[:, columns])
-        planes = const.tile([P, PASSES // PLANES, N_ALL], U8, align_bytes=64)
-        load_weight_scales(nc, planes, W_qkv_scales)
-
         identity = const.tile([P, P], F32)
         make_identity(nc, identity[:])
+        planes = const.tile([P, PASSES // PLANES, N_ALL], U8, align_bytes=64)
+        load_weight_scales(nc, planes, W_qkv_scales)
         cos_sin = const.tile([P, 2, PAIRS], F32)
         make_cos_sin(nc, const, cos_sin)
 

@@ -27,6 +27,7 @@ V_KIND = 2
 N_ALL = 3072
 BANK = 512
 BANKS = N_ALL // BANK
+HEADS_IN_BANK = BANK // HEAD
 PLANES = 4
 QUADRANTS = 4
 ROUND_MAGIC = 1.5 * 2.0**23
@@ -80,20 +81,30 @@ def make_cos_sin(nc, const, cos_sin):
     nc.scalar.activation(out=cos_sin[:], in_=part_turn[:], func=ACT.Sin, scale=2.0 * math.pi)
 
 
-def rotate(nc, work, segment, cos_sin):
-    heads = SEGMENT // HEAD
-    x = segment.rearrange("p (h d) -> p h d", d=HEAD)[:, :, 0:ROT].rearrange(
-        "p h (j e) -> p h j e", e=2
-    )
-    shape = [P, heads, PAIRS, 2]
+def make_rotation_table(nc, table, cos_sin):
+    shape = [P, HEADS_IN_BANK, PAIRS, 2]
     cos = cos_sin[:, COS, :].unsqueeze(1).unsqueeze(3).to_broadcast(shape)
-    sin = cos_sin[:, SIN, :].unsqueeze(1).unsqueeze(3).to_broadcast(shape)
-    x_cos = work.tile(shape, F32)
-    x_sin = work.tile(shape, F32)
-    nc.vector.tensor_mul(out=x_cos[:], in0=x, in1=cos)
-    nc.vector.tensor_mul(out=x_sin[:], in0=x, in1=sin)
-    nc.vector.tensor_sub(out=x[:, :, :, 0], in0=x_cos[:, :, :, 0], in1=x_sin[:, :, :, 1])
-    nc.vector.tensor_add(out=x[:, :, :, 1], in0=x_cos[:, :, :, 1], in1=x_sin[:, :, :, 0])
+    nc.vector.tensor_copy(out=table[:, 0, :, :].rearrange("p h (j e) -> p h j e", e=2), in_=cos)
+    sin = cos_sin[:, SIN, :].unsqueeze(1).to_broadcast([P, HEADS_IN_BANK, PAIRS])
+    by_pair = table[:, 1, :, :].rearrange("p h (j e) -> p h j e", e=2)
+    nc.vector.tensor_copy(out=by_pair[:, :, :, 0], in_=sin)
+    nc.vector.tensor_scalar_mul(out=by_pair[:, :, :, 1], in0=sin, scalar1=-1.0)
+
+
+def rotate(nc, work, heads_psum, heads_out, table):
+    heads = heads_psum.shape[1]
+    shape = [P, 2, heads, ROT]
+    products = work.tile([P, 2, HEADS_IN_BANK, ROT], F32)
+    nc.vector.tensor_mul(
+        out=products[:, :, 0:heads, :],
+        in0=heads_psum[:, :, 0:ROT].unsqueeze(1).to_broadcast(shape),
+        in1=table[:, :, 0:heads, :],
+    )
+    x_cos = products[:, 0, 0:heads, :].rearrange("p h (j e) -> p h j e", e=2)
+    x_sin = products[:, 1, 0:heads, :].rearrange("p h (j e) -> p h j e", e=2)
+    y = heads_out[:, :, 0:ROT].rearrange("p h (j e) -> p h j e", e=2)
+    nc.vector.tensor_add(out=y[:, :, :, 0], in0=x_cos[:, :, :, 0], in1=x_sin[:, :, :, 1])
+    nc.vector.tensor_add(out=y[:, :, :, 1], in0=x_cos[:, :, :, 1], in1=x_sin[:, :, :, 0])
 
 
 def tile_progenattention_pa_k_kernel(
@@ -108,7 +119,7 @@ def tile_progenattention_pa_k_kernel(
         stage = pools.enter_context(tc.tile_pool(name="stage", bufs=3))
         w_pool = pools.enter_context(tc.tile_pool(name="w", bufs=8))
         last_pool = pools.enter_context(tc.tile_pool(name="last", bufs=BANKS))
-        result_pool = pools.enter_context(tc.tile_pool(name="result", bufs=2 * BANKS))
+        result_pool = pools.enter_context(tc.tile_pool(name="result", bufs=BANKS))
         work = pools.enter_context(tc.tile_pool(name="work", bufs=4))
         psum = pools.enter_context(tc.psum_pool(name="psum", bufs=8))
 
@@ -123,6 +134,8 @@ def tile_progenattention_pa_k_kernel(
         load_weight_scales(nc, planes, W_qkv_scales)
         cos_sin = const.tile([P, 2, PAIRS], F32)
         make_cos_sin(nc, const, cos_sin)
+        table = const.tile([P, 2, HEADS_IN_BANK, ROT], F32)
+        make_rotation_table(nc, table, cos_sin)
 
         x_words = x_sb[:].bitcast(F32)
         x_codes = const.tile([P, PASSES * P], U32, align_bytes=64)
@@ -186,14 +199,23 @@ def tile_progenattention_pa_k_kernel(
             )
             last_codes.append(piece)
 
+        segments_in_bank = BANK // SEGMENT
         for b in range(BANKS):
             mx_pass(PASSES - 1, b, last_codes[b][:])
-            for s in range(BANK // SEGMENT):
-                group, kind = divmod(b * (BANK // SEGMENT) + s, KINDS)
-                segment = result_pool.tile([P, SEGMENT], F32)
-                nc.scalar.copy(out=segment[:], in_=banks[b][:, SEGMENT * s : SEGMENT * (s + 1)])
-                if kind != V_KIND:
-                    rotate(nc, work, segment[:], cos_sin)
+            result = result_pool.tile([P, BANK], F32)
+            kinds = [(b * segments_in_bank + s) % KINDS for s in range(segments_in_bank)]
+            rotated = [s for s in range(segments_in_bank) if kinds[s] != V_KIND]
+            columns = slice(SEGMENT * rotated[0], SEGMENT * (rotated[-1] + 1))
+            heads_psum = banks[b][:, columns].rearrange("p (h d) -> p h d", d=HEAD)
+            heads_out = result[:, columns].rearrange("p (h d) -> p h d", d=HEAD)
+            rotate(nc, work, heads_psum, heads_out, table)
+            nc.scalar.copy(out=heads_out[:, :, ROT:HEAD], in_=heads_psum[:, :, ROT:HEAD])
+            for s in range(segments_in_bank):
+                group = (b * segments_in_bank + s) // KINDS
+                columns = slice(SEGMENT * s, SEGMENT * (s + 1))
+                if kinds[s] == V_KIND:
+                    nc.scalar.copy(out=result[:, columns], in_=banks[b][:, columns])
                 nc.sync.dma_start(
-                    out=outs[kind][:, SEGMENT * group : SEGMENT * (group + 1)], in_=segment[:]
+                    out=outs[kinds[s]][:, SEGMENT * group : SEGMENT * (group + 1)],
+                    in_=result[:, columns],
                 )

@@ -37,17 +37,20 @@ SIN = 1
 FLOPS = 2 * P * E * N_ALL
 
 
+def scale_views(planes, w_scales, j, quadrant, dtype):
+    first = 32 * quadrant
+    return (
+        planes[first : first + 4 * PLANES, j, :].bitcast(dtype),
+        w_scales[PLANES * j : PLANES * (j + 1), 4 * quadrant : 4 * (quadrant + 1), :].bitcast(dtype),
+    )
+
+
 def load_weight_scales(nc, planes, w_scales):
     nc.vector.memset(planes[:].rearrange("p j n -> p (j n)").bitcast(I32), 0)
     for j in range(PASSES // PLANES):
-        for quadrant in range(QUADRANTS):
-            first = 32 * quadrant
-            nc.gpsimd.dma_start(
-                out=planes[first : first + 4 * PLANES, j, :].bitcast(F32),
-                in_=w_scales[
-                    PLANES * j : PLANES * (j + 1), 4 * quadrant : 4 * (quadrant + 1), :
-                ].bitcast(F32),
-            )
+        for quadrant in (2, 3):
+            out, in_ = scale_views(planes, w_scales, j, quadrant, F32)
+            nc.gpsimd.dma_start(out=out, in_=in_)
 
 
 def make_cos_sin(nc, const, cos_sin):
@@ -181,6 +184,10 @@ def tile_progenattention_pa_k_kernel(
             )
 
         for g in range(PASSES - 1):
+            if g % PLANES == 0:
+                for quadrant in (0, 1):
+                    out, in_ = scale_views(planes, W_qkv_scales, g // PLANES, quadrant, I32)
+                    nc.sync.dma_start(out=out, in_=in_)
             w_codes = w_pool.tile([P, N_ALL], U32, align_bytes=64)
             nc.sync.dma_start(
                 out=w_codes[:].bitcast(I32),

@@ -26,8 +26,9 @@ KINDS = 3
 V_KIND = 2
 N_ALL = 3072
 BANK = 512
-BANKS = N_ALL // BANK
 HEADS_IN_BANK = BANK // HEAD
+GROUP = KINDS * SEGMENT
+GROUPS = N_ALL // GROUP
 PLANES = 4
 QUADRANTS = 4
 ROUND_MAGIC = 1.5 * 2.0**23
@@ -95,19 +96,17 @@ def make_rotation_table(nc, table, cos_sin):
 
 
 def rotate(nc, work, heads_psum, heads_out, table):
-    heads = heads_psum.shape[1]
-    shape = [P, 2, heads, ROT]
     products = work.tile([P, 2, HEADS_IN_BANK, ROT], F32)
     nc.vector.tensor_mul(
-        out=products[:, :, 0:heads, :],
-        in0=heads_psum[:, :, 0:ROT].unsqueeze(1).to_broadcast(shape),
-        in1=table[:, :, 0:heads, :],
+        out=products[:],
+        in0=heads_psum[:, :, 0:ROT].unsqueeze(1).to_broadcast([P, 2, HEADS_IN_BANK, ROT]),
+        in1=table[:],
     )
-    x_cos = products[:, 0, 0:heads, :].rearrange("p h (j e) -> p h j e", e=2)
-    x_sin = products[:, 1, 0:heads, :].rearrange("p h (j e) -> p h j e", e=2)
-    y = heads_out[:, :, 0:ROT].rearrange("p h (j e) -> p h j e", e=2)
-    nc.vector.tensor_add(out=y[:, :, :, 0], in0=x_cos[:, :, :, 0], in1=x_sin[:, :, :, 1])
-    nc.vector.tensor_add(out=y[:, :, :, 1], in0=x_cos[:, :, :, 1], in1=x_sin[:, :, :, 0])
+    x_cos = products[:, 0, :, :].rearrange("p (s h) (j e) -> p s h j e", s=2, e=2)
+    x_sin = products[:, 1, :, :].rearrange("p (s h) (j e) -> p s h j e", s=2, e=2)
+    y = heads_out[:, :, :, 0:ROT].rearrange("p s h (j e) -> p s h j e", e=2)
+    nc.vector.tensor_add(out=y[:, :, :, :, 0], in0=x_cos[:, :, :, :, 0], in1=x_sin[:, :, :, :, 1])
+    nc.vector.tensor_add(out=y[:, :, :, :, 1], in0=x_cos[:, :, :, :, 1], in1=x_sin[:, :, :, :, 0])
 
 
 def tile_progenattention_pa_k_kernel(
@@ -121,8 +120,8 @@ def tile_progenattention_pa_k_kernel(
         const = pools.enter_context(tc.tile_pool(name="const", bufs=1))
         stage = pools.enter_context(tc.tile_pool(name="stage", bufs=3))
         w_pool = pools.enter_context(tc.tile_pool(name="w", bufs=8))
-        last_pool = pools.enter_context(tc.tile_pool(name="last", bufs=BANKS))
-        result_pool = pools.enter_context(tc.tile_pool(name="result", bufs=BANKS))
+        last_pool = pools.enter_context(tc.tile_pool(name="last", bufs=GROUPS))
+        result_pool = pools.enter_context(tc.tile_pool(name="result", bufs=2))
         work = pools.enter_context(tc.tile_pool(name="work", bufs=4))
         psum = pools.enter_context(tc.psum_pool(name="psum", bufs=8))
 
@@ -166,22 +165,28 @@ def tile_progenattention_pa_k_kernel(
                 in_=grouped[:],
             )
 
-        banks = []
-        for b in range(BANKS):
-            banks.append(psum.tile([P, BANK], F32, tag="bank", name="qkv_bank%d" % b))
+        qk_banks = []
+        v_banks = []
+        for c in range(GROUPS):
+            qk_banks.append(psum.tile([P, 2 * SEGMENT], F32, tag="bank", name="qk_bank%d" % c))
+            v_banks.append(psum.tile([P, SEGMENT], F32, tag="bank", name="v_bank%d" % c))
 
-        def mx_pass(g, b, w_codes):
+        def mx_pass(g, bank, first_column, width, w_codes):
             j, i = divmod(g, PLANES)
             tokens = slice(P * g, P * (g + 1))
             nc.tensor.matmul_mx(
-                out=banks[b][:],
+                out=bank[:],
                 lhsT=x_codes[:, tokens].bitcast(FP8X4),
                 lhsT_scale=x_scales[:, tokens],
                 rhs=w_codes.bitcast(FP8X4),
-                rhs_scale=planes[4 * i : P, j, BANK * b : BANK * (b + 1)],
+                rhs_scale=planes[4 * i : P, j, first_column : first_column + width],
                 start=(g == 0),
                 stop=(g == PASSES - 1),
             )
+
+        def mx_group(g, c, w_codes):
+            mx_pass(g, qk_banks[c], GROUP * c, 2 * SEGMENT, w_codes[:, 0 : 2 * SEGMENT])
+            mx_pass(g, v_banks[c], GROUP * c + 2 * SEGMENT, SEGMENT, w_codes[:, 2 * SEGMENT : GROUP])
 
         for g in range(PASSES - 1):
             if g % PLANES == 0:
@@ -193,36 +198,36 @@ def tile_progenattention_pa_k_kernel(
                 out=w_codes[:].bitcast(I32),
                 in_=W_qkv_words[g].rearrange("p n t -> p (n t)").bitcast(I32),
             )
-            for b in range(BANKS):
-                mx_pass(g, b, w_codes[:, BANK * b : BANK * (b + 1)])
+            for c in range(GROUPS):
+                mx_group(g, c, w_codes[:, GROUP * c : GROUP * (c + 1)])
 
         last_bytes = W_qkv_words[PASSES - 1].rearrange("p n t -> p (n t)")
         last_codes = []
-        for b in range(BANKS):
-            piece = last_pool.tile([P, BANK], U32, align_bytes=64, name="piece%d" % b, tag="piece")
+        for c in range(GROUPS):
+            piece = last_pool.tile([P, GROUP], U32, align_bytes=64, name="piece%d" % c, tag="piece")
             nc.sync.dma_start(
                 out=piece[:].bitcast(I32),
-                in_=last_bytes[:, 4 * BANK * b : 4 * BANK * (b + 1)].bitcast(I32),
+                in_=last_bytes[:, 4 * GROUP * c : 4 * GROUP * (c + 1)].bitcast(I32),
             )
             last_codes.append(piece)
 
-        segments_in_bank = BANK // SEGMENT
-        for b in range(BANKS):
-            mx_pass(PASSES - 1, b, last_codes[b][:])
-            result = result_pool.tile([P, BANK], F32)
-            kinds = [(b * segments_in_bank + s) % KINDS for s in range(segments_in_bank)]
-            rotated = [s for s in range(segments_in_bank) if kinds[s] != V_KIND]
-            columns = slice(SEGMENT * rotated[0], SEGMENT * (rotated[-1] + 1))
-            heads_psum = banks[b][:, columns].rearrange("p (h d) -> p h d", d=HEAD)
-            heads_out = result[:, columns].rearrange("p (h d) -> p h d", d=HEAD)
+        for c in range(GROUPS):
+            mx_group(PASSES - 1, c, last_codes[c][:])
+            low = c % 2
+            if low == 0:
+                result = result_pool.tile([P, KINDS, 2, SEGMENT], F32)
+            heads_psum = qk_banks[c][:].rearrange("p (h d) -> p h d", d=HEAD)
+            heads_out = result[:, 0:V_KIND, low, :].rearrange("p s (h d) -> p s h d", d=HEAD)
             rotate(nc, work, heads_psum, heads_out, table)
-            nc.scalar.copy(out=heads_out[:, :, ROT:HEAD], in_=heads_psum[:, :, ROT:HEAD])
-            for s in range(segments_in_bank):
-                group = (b * segments_in_bank + s) // KINDS
-                columns = slice(SEGMENT * s, SEGMENT * (s + 1))
-                if kinds[s] == V_KIND:
-                    nc.scalar.copy(out=result[:, columns], in_=banks[b][:, columns])
-                nc.sync.dma_start(
-                    out=outs[kinds[s]][:, SEGMENT * group : SEGMENT * (group + 1)],
-                    in_=result[:, columns],
-                )
+            nc.scalar.copy(out=result[:, V_KIND, low, :], in_=v_banks[c][:])
+            nc.scalar.copy(
+                out=heads_out[:, :, :, ROT:HEAD],
+                in_=qk_banks[c][:].rearrange("p (s h d) -> p s h d", s=2, d=HEAD)[:, :, :, ROT:HEAD],
+            )
+            if low == 1:
+                columns = slice(SEGMENT * (c - 1), SEGMENT * (c + 1))
+                for kind in (V_KIND, 0, 1):
+                    nc.sync.dma_start(
+                        out=outs[kind][:, columns],
+                        in_=result[:, kind, :, :].rearrange("p c n -> p (c n)"),
+                    )

@@ -120,7 +120,7 @@ def tile_progenattention_pa_k_kernel(
         const = pools.enter_context(tc.tile_pool(name="const", bufs=1))
         stage = pools.enter_context(tc.tile_pool(name="stage", bufs=3))
         w_pool = pools.enter_context(tc.tile_pool(name="w", bufs=8))
-        last_pool = pools.enter_context(tc.tile_pool(name="last", bufs=GROUPS))
+        last_pool = pools.enter_context(tc.tile_pool(name="last", bufs=GROUPS // 2))
         result_pool = pools.enter_context(tc.tile_pool(name="result", bufs=2))
         work = pools.enter_context(tc.tile_pool(name="work", bufs=4))
         psum = pools.enter_context(tc.psum_pool(name="psum", bufs=8))
@@ -203,17 +203,17 @@ def tile_progenattention_pa_k_kernel(
 
         last_bytes = W_qkv_words[PASSES - 1].rearrange("p n t -> p (n t)")
         last_codes = []
-        for c in range(GROUPS):
-            piece = last_pool.tile([P, GROUP], U32, align_bytes=64, name="piece%d" % c, tag="piece")
+        for i in range(GROUPS // 2):
+            piece = last_pool.tile([P, 2 * GROUP], U32, align_bytes=64, name="piece%d" % i, tag="piece")
             nc.sync.dma_start(
                 out=piece[:].bitcast(I32),
-                in_=last_bytes[:, 4 * GROUP * c : 4 * GROUP * (c + 1)].bitcast(I32),
+                in_=last_bytes[:, 4 * 2 * GROUP * i : 4 * 2 * GROUP * (i + 1)].bitcast(I32),
             )
             last_codes.append(piece)
 
         for c in range(GROUPS):
-            mx_group(PASSES - 1, c, last_codes[c][:])
             low = c % 2
+            mx_group(PASSES - 1, c, last_codes[c // 2][:, GROUP * low : GROUP * (low + 1)])
             if low == 0:
                 result = result_pool.tile([P, KINDS, 2, SEGMENT], F32)
             heads_psum = qk_banks[c][:].rearrange("p (h d) -> p h d", d=HEAD)

import math
from contextlib import ExitStack

import concourse.mybir as mybir
from concourse.masks import make_identity

F32 = mybir.dt.float32
BF16 = mybir.dt.bfloat16
I32 = mybir.dt.int32
U32 = mybir.dt.uint32
U8 = mybir.dt.uint8
FP8X4 = mybir.dt.float8_e4m3fn_x4
ALU = mybir.AluOpType
ACT = mybir.ActivationFunctionType

P = 128
POSITIONS = 64
E = 8192
K_PASS = 512
PASSES = E // K_PASS
HEAD = 128
ROT = 32
PAIRS = ROT // 2
SEGMENT = 256
KINDS = 3
V_KIND = 2
N_ALL = 3072
BANK = 512
HEADS_IN_BANK = BANK // HEAD
GROUP = KINDS * SEGMENT
GROUPS = N_ALL // GROUP
PLANES = 4
QUADRANTS = 4
ROUND_MAGIC = 1.5 * 2.0**23
COS = 0
SIN = 1

FLOPS = 2 * P * E * N_ALL


def scale_views(planes, w_scales, j, quadrant, dtype):
    first = 32 * quadrant
    return (
        planes[first : first + 4 * PLANES, j, :].bitcast(dtype),
        w_scales[PLANES * j : PLANES * (j + 1), 4 * quadrant : 4 * (quadrant + 1), :].bitcast(dtype),
    )


def load_weight_scales(nc, planes, w_scales):
    nc.vector.memset(planes[:].rearrange("p j n -> p (j n)").bitcast(I32), 0)
    for j in range(PASSES // PLANES):
        for quadrant in (2, 3):
            out, in_ = scale_views(planes, w_scales, j, quadrant, F32)
            nc.gpsimd.dma_start(out=out, in_=in_)


def make_cos_sin(nc, const, cos_sin):
    token = const.tile([P, 1], I32)
    nc.gpsimd.iota(token[:], pattern=[[0, 1]], base=0, channel_multiplier=1)
    position_int = const.tile([P, 1], I32)
    nc.vector.tensor_single_scalar(
        out=position_int[:], in_=token[:], scalar=POSITIONS - 1, op=ALU.bitwise_and
    )
    position = const.tile([P, 1], F32)
    nc.vector.tensor_copy(out=position[:], in_=position_int[:])

    turns = const.tile([P, 2, PAIRS], F32)
    for j in range(PAIRS):
        turns_per_position = 10000.0 ** (-2.0 * j / ROT) / (2.0 * math.pi)
        nc.vector.tensor_scalar_mul(
            out=turns[:, SIN, j : j + 1], in0=position[:], scalar1=turns_per_position
        )
    nc.vector.tensor_scalar_add(out=turns[:, COS, :], in0=turns[:, SIN, :], scalar1=0.25)
    whole_turns = const.tile([P, 2, PAIRS], F32)
    nc.vector.tensor_scalar(
        out=whole_turns[:],
        in0=turns[:],
        scalar1=ROUND_MAGIC,
        scalar2=ROUND_MAGIC,
        op0=ALU.add,
        op1=ALU.subtract,
    )
    part_turn = const.tile([P, 2, PAIRS], F32)
    nc.vector.tensor_sub(out=part_turn[:], in0=turns[:], in1=whole_turns[:])
    nc.scalar.activation(out=cos_sin[:], in_=part_turn[:], func=ACT.Sin, scale=2.0 * math.pi)


def make_rotation_table(nc, table, cos_sin):
    shape = [P, HEADS_IN_BANK, PAIRS, 2]
    cos = cos_sin[:, COS, :].unsqueeze(1).unsqueeze(3).to_broadcast(shape)
    nc.vector.tensor_copy(out=table[:, 0, :, :].rearrange("p h (j e) -> p h j e", e=2), in_=cos)
    sin = cos_sin[:, SIN, :].unsqueeze(1).to_broadcast([P, HEADS_IN_BANK, PAIRS])
    by_pair = table[:, 1, :, :].rearrange("p h (j e) -> p h j e", e=2)
    nc.vector.tensor_copy(out=by_pair[:, :, :, 0], in_=sin)
    nc.vector.tensor_scalar_mul(out=by_pair[:, :, :, 1], in0=sin, scalar1=-1.0)


def rotate(nc, work, heads_psum, heads_out, table):
    products = work.tile([P, 2, HEADS_IN_BANK, ROT], F32)
    nc.vector.tensor_mul(
        out=products[:],
        in0=heads_psum[:, :, 0:ROT].unsqueeze(1).to_broadcast([P, 2, HEADS_IN_BANK, ROT]),
        in1=table[:],
    )
    x_cos = products[:, 0, :, :].rearrange("p (s h) (j e) -> p s h j e", s=2, e=2)
    x_sin = products[:, 1, :, :].rearrange("p (s h) (j e) -> p s h j e", s=2, e=2)
    y = heads_out[:, :, :, 0:ROT].rearrange("p s h (j e) -> p s h j e", e=2)
    nc.vector.tensor_add(out=y[:, :, :, :, 0], in0=x_cos[:, :, :, :, 0], in1=x_sin[:, :, :, :, 1])
    nc.vector.tensor_add(out=y[:, :, :, :, 1], in0=x_cos[:, :, :, :, 1], in1=x_sin[:, :, :, :, 0])


def tile_progenattention_pa_k_kernel(
    tc, hidden_states, W_qkv_words, W_qkv_scales, out_0, out_1, out_2
):
    nc = tc.nc
    x_dram = hidden_states.flatten_outer_dims()
    outs = [out.rearrange("b s h d -> (b s) (h d)") for out in (out_0, out_1, out_2)]

    with ExitStack() as pools:
        const = pools.enter_context(tc.tile_pool(name="const", bufs=1))
        stage = pools.enter_context(tc.tile_pool(name="stage", bufs=3))
        w_pool = pools.enter_context(tc.tile_pool(name="w", bufs=8))
        last_pool = pools.enter_context(tc.tile_pool(name="last", bufs=GROUPS // 2))
        result_pool = pools.enter_context(tc.tile_pool(name="result", bufs=2))
        work = pools.enter_context(tc.tile_pool(name="work", bufs=4))
        psum = pools.enter_context(tc.psum_pool(name="psum", bufs=8))

        x_sb = const.tile([P, E], BF16)
        half = E // 2
        for i in range(2):
            columns = slice(half * i, half * (i + 1))
            nc.sync.dma_start(out=x_sb[:, columns], in_=x_dram[:, columns])
        identity = const.tile([P, P], F32)
        make_identity(nc, identity[:])
        planes = const.tile([P, PASSES // PLANES, N_ALL], U8, align_bytes=64)
        load_weight_scales(nc, planes, W_qkv_scales)
        cos_sin = const.tile([P, 2, PAIRS], F32)
        make_cos_sin(nc, const, cos_sin)
        table = const.tile([P, 2, HEADS_IN_BANK, ROT], F32)
        make_rotation_table(nc, table, cos_sin)

        x_words = x_sb[:].bitcast(F32)
        x_codes = const.tile([P, PASSES * P], U32, align_bytes=64)
        x_scales = const.tile([P, PASSES * P], U8, align_bytes=64)
        words_in_pass = K_PASS // 2
        for i in range(PASSES // 2):
            transposed = psum.tile([P, 2, 2, P], F32, tag="bank")
            for g_low in range(2):
                first_word = words_in_pass * (2 * i + g_low)
                for u in range(2):
                    nc.tensor.transpose(
                        transposed[:, g_low, u, :],
                        x_words[:, first_word + u : first_word + words_in_pass : 2],
                        identity[:],
                    )
            grouped = stage.tile([P, 2 * K_PASS], BF16, align_bytes=64)
            nc.scalar.copy(
                out=grouped[:].bitcast(F32).rearrange("p (g r u) -> p g r u", g=2, u=2),
                in_=transposed[:].rearrange("p g u r -> p g r u"),
            )
            tokens_of_two_passes = slice(2 * P * i, 2 * P * (i + 1))
            nc.vector.quantize_mx(
                out=x_codes[:, tokens_of_two_passes].bitcast(FP8X4),
                scales=x_scales[:, tokens_of_two_passes],
                in_=grouped[:],
            )

        qk_banks = []
        v_banks = []
        for c in range(GROUPS):
            qk_banks.append(psum.tile([P, 2 * SEGMENT], F32, tag="bank", name="qk_bank%d" % c))
            v_banks.append(psum.tile([P, SEGMENT], F32, tag="bank", name="v_bank%d" % c))

        def mx_pass(g, bank, first_column, width, w_codes):
            j, i = divmod(g, PLANES)
            tokens = slice(P * g, P * (g + 1))
            nc.tensor.matmul_mx(
                out=bank[:],
                lhsT=x_codes[:, tokens].bitcast(FP8X4),
                lhsT_scale=x_scales[:, tokens],
                rhs=w_codes.bitcast(FP8X4),
                rhs_scale=planes[4 * i : P, j, first_column : first_column + width],
                start=(g == 0),
                stop=(g == PASSES - 1),
            )

        def mx_group(g, c, w_codes):
            mx_pass(g, qk_banks[c], GROUP * c, 2 * SEGMENT, w_codes[:, 0 : 2 * SEGMENT])
            mx_pass(g, v_banks[c], GROUP * c + 2 * SEGMENT, SEGMENT, w_codes[:, 2 * SEGMENT : GROUP])

        for g in range(PASSES - 1):
            if g % PLANES == 0:
                for quadrant in (0, 1):
                    out, in_ = scale_views(planes, W_qkv_scales, g // PLANES, quadrant, I32)
                    nc.sync.dma_start(out=out, in_=in_)
            w_codes = w_pool.tile([P, N_ALL], U32, align_bytes=64)
            nc.sync.dma_start(
                out=w_codes[:].bitcast(I32),
                in_=W_qkv_words[g].rearrange("p n t -> p (n t)").bitcast(I32),
            )
            for c in range(GROUPS):
                mx_group(g, c, w_codes[:, GROUP * c : GROUP * (c + 1)])

        last_bytes = W_qkv_words[PASSES - 1].rearrange("p n t -> p (n t)")
        last_codes = []
        for i in range(GROUPS // 2):
            piece = last_pool.tile([P, 2 * GROUP], U32, align_bytes=64, name="piece%d" % i, tag="piece")
            nc.sync.dma_start(
                out=piece[:].bitcast(I32),
                in_=last_bytes[:, 4 * 2 * GROUP * i : 4 * 2 * GROUP * (i + 1)].bitcast(I32),
            )
            last_codes.append(piece)

        for c in range(GROUPS):
            low = c % 2
            mx_group(PASSES - 1, c, last_codes[c // 2][:, GROUP * low : GROUP * (low + 1)])
            if low == 0:
                result = result_pool.tile([P, KINDS, 2, SEGMENT], F32)
            heads_psum = qk_banks[c][:].rearrange("p (h d) -> p h d", d=HEAD)
            heads_out = result[:, 0:V_KIND, low, :].rearrange("p s (h d) -> p s h d", d=HEAD)
            rotate(nc, work, heads_psum, heads_out, table)
            nc.scalar.copy(out=result[:, V_KIND, low, :], in_=v_banks[c][:])
            nc.scalar.copy(
                out=heads_out[:, :, :, ROT:HEAD],
                in_=qk_banks[c][:].rearrange("p (s h d) -> p s h d", s=2, d=HEAD)[:, :, :, ROT:HEAD],
            )
            if low == 1:
                columns = slice(SEGMENT * (c - 1), SEGMENT * (c + 1))
                for kind in (V_KIND, 0, 1):
                    nc.sync.dma_start(
                        out=outs[kind][:, columns],
                        in_=result[:, kind, :, :].rearrange("p c n -> p (c n)"),
                    )
